import numpy as np
import ml_dtypes


def mxq(x, axis, fmt="e4m3"):
    dtype, down = {"e4m3": (ml_dtypes.float8_e4m3fn, 7), "e5m2": (ml_dtypes.float8_e5m2, 14)}[fmt]
    v = np.moveaxis(np.asarray(x, np.float32).astype(ml_dtypes.bfloat16).astype(np.float64), axis, -1)
    blocks = v.reshape(v.shape[:-1] + (-1, 32))
    amax = np.abs(blocks).max(-1, keepdims=True)
    byte = np.maximum(np.where(amax > 0, np.frexp(amax)[1] - 1 + 127, 0) - down, 1)
    scale = np.exp2(byte - 127.0)
    codes = (blocks / scale).astype(np.float32).astype(dtype).astype(np.float64)
    return np.moveaxis((codes * scale).reshape(v.shape), -1, axis)


WIDE = False


def mx_kscale(k):
    if not WIDE:
        return np.ones(k)
    levels = np.array([10, -10, 5, -5, 0])
    if k % 512:
        return np.exp2(np.random.permutation(np.resize(levels, k // 32))).repeat(32)
    a = np.empty((k // 512, 16))
    for p in range(k // 512):
        a[p, :8] = np.random.permutation(np.resize(levels, 8))
        for g in range(8):
            far = levels[np.abs(levels - a[p, g]) >= 10]
            a[p, g + 8] = far[np.random.randint(len(far))]
    return np.exp2(a.ravel()).repeat(32)


BF16 = ml_dtypes.bfloat16


def bf(x):
    return np.asarray(x, np.float32).astype(BF16)


def f64(x):
    return np.asarray(x).astype(np.float64)


B, S, NH, HD = 1, 512, 4, 128
H = NH * HD


def split_heads(x):
    return x.reshape(B, S, NH, HD).transpose(0, 2, 1, 3)


def setup_inputs():
    t = mx_kscale(S)
    t = t / t.max()
    kind = np.random.randint(0, 4, (B, S))
    base = np.where(kind < 2, 0.0, np.where(kind == 2, -10000.0, np.random.standard_normal((B, S))))
    return {"model_hidden_states": bf(np.random.standard_normal((B, S, H))),
            "k_hidden_states": bf(np.random.standard_normal((B, S, H))),
            "k_embeddings": bf(np.random.standard_normal((B, S, H)) * 0.15 * np.sqrt(S) / t[None, :, None]),
            "attention_mask": bf(base + np.log(t)[None, :])}


def reference(model_hidden_states, k_hidden_states, k_embeddings, attention_mask):
    q = split_heads(f64(model_hidden_states))
    k = split_heads(f64(k_hidden_states))
    v = split_heads(f64(k_embeddings))
    energy = q @ k.transpose(0, 1, 3, 2) / np.sqrt(HD)
    m = f64(attention_mask)[:, None, None, :]
    energy = np.where(m == 0, energy, m)
    e = np.exp(energy - energy.max(-1, keepdims=True))
    attn = (mxq(e, 3, "e4m3") @ mxq(v, 2, "e4m3")) / e.sum(-1, keepdims=True)
    return attn.transpose(0, 2, 1, 3).reshape(B, S, H)

@@ -1,0 +1,247 @@
+import math
+
+import concourse.mybir as mybir
+from concourse.masks import make_identity
+
+BF16 = mybir.dt.bfloat16
+F32 = mybir.dt.float32
+U32 = mybir.dt.uint32
+U8 = mybir.dt.uint8
+FP8X4 = mybir.dt.float8_e4m3fn_x4
+ALU = mybir.AluOpType
+ACT = mybir.ActivationFunctionType
+
+P = 128
+S = 512
+HEADS = 4
+HD = 128
+TOKEN_TILES = S // P
+TILES = HEADS * TOKEN_TILES
+PACK = 4
+SCALE = 1.0 / math.sqrt(HD)
+V_ROUND = 2
+
+FLOPS = 2 * (2 * HEADS * S * S * HD)
+
+
+def tile_knnattention_s_kernel(
+    tc, model_hidden_states, k_hidden_states, k_embeddings, attention_mask, out
+):
+    nc = tc.nc
+    q_dram = model_hidden_states.flatten_outer_dims().rearrange("(t p) c -> p t c", p=P)
+    k_dram = k_hidden_states.flatten_outer_dims().rearrange("(t p) c -> p t c", p=P)
+    out_dram = out.flatten_outer_dims().rearrange("(t p) c -> p t c", p=P)
+    v_dram = k_embeddings.flatten_outer_dims().rearrange("(p j) c -> p (j c)", j=PACK)
+
+    with (
+        tc.tile_pool(name="const", bufs=1) as const,
+        tc.tile_pool(name="work", bufs=4) as work,
+        tc.tile_pool(name="small", bufs=8) as small,
+        tc.psum_pool(name="psum_prep", bufs=1) as psum_prep,
+        tc.psum_pool(name="psum_s", bufs=3) as psum_s,
+        tc.psum_pool(name="psum_eT", bufs=2) as psum_eT,
+        tc.psum_pool(name="psum_acc", bufs=2) as psum_acc,
+        tc.manual_schedule(),
+    ):
+        mask_row = const.tile([P, S], BF16)
+        nc.gpsimd.memset(mask_row[:].bitcast(F32), 0.0)
+        nc.sync.dma_start(out=mask_row[0:1, :], in_=attention_mask)
+        q_sb = []
+        k_sb = []
+        v_raw = const.tile([P, PACK, S], BF16)
+        for h in range(HEADS):
+            head_cols = slice(h * HD, (h + 1) * HD)
+            q_h = const.tile([P, TOKEN_TILES, HD], BF16, name="q_sb%d" % h)
+            nc.sync.dma_start(out=q_h[:], in_=q_dram[:, :, head_cols])
+            q_sb.append(q_h)
+            k_h = const.tile([P, TOKEN_TILES, HD], BF16, name="k_sb%d" % h)
+            nc.sync.dma_start(out=k_h[:], in_=k_dram[:, :, head_cols])
+            k_sb.append(k_h)
+            if h == 0:
+                nc.sync.dma_start(
+                    out=v_raw[:].rearrange("p j c -> p (j c)"), in_=v_dram
+                )
+
+        ident_bf = const.tile([P, P], BF16)
+        make_identity(nc, ident_bf[:])
+        ident_f32 = const.tile([P, P], F32)
+        make_identity(nc, ident_f32[:])
+        ones = const.tile([P, P], BF16)
+        nc.vector.memset(ones[:], 1.0)
+        warm = const.tile([P, 1], F32)
+        nc.vector.memset(warm[:], 0.0)
+        nc.scalar.activation(out=warm[:], in_=warm[:], func=ACT.Exp)
+
+        mask_ps = psum_acc.tile([P, TOKEN_TILES, P], F32, tag="acc")
+        for t in range(TOKEN_TILES):
+            nc.tensor.matmul(
+                mask_ps[:, t, :], lhsT=mask_row[:, t * P : (t + 1) * P], rhs=ones[:],
+                start=True, stop=True,
+            )
+        ident_kept = const.tile([P, TOKEN_TILES, P], BF16)
+        nc.vector.scalar_tensor_tensor(
+            out=ident_kept[:],
+            in0=mask_ps[:],
+            scalar=0.0,
+            in1=ident_bf[:].unsqueeze(1).to_broadcast([P, TOKEN_TILES, P]),
+            op0=ALU.is_equal,
+            op1=ALU.mult,
+        )
+        mask_cols = const.tile([P, TOKEN_TILES, P], F32)
+        nc.vector.tensor_scalar_mul(out=mask_cols[:], in0=mask_ps[:], scalar1=math.sqrt(HD))
+
+        v_grouped = const.tile([P, S, PACK], BF16, align_bytes=64)
+        v_codes = const.tile([P, S], U32, align_bytes=64)
+        v_scales = const.tile([P, S], U8, align_bytes=64)
+
+        def quantise_v():
+            nc.vector.tensor_copy(
+                out=v_grouped[:], in_=v_raw[:].rearrange("p t c -> p c t")
+            )
+            nc.vector.quantize_mx(
+                out=v_codes[:].bitcast(FP8X4),
+                scales=v_scales[:],
+                in_=v_grouped[:].rearrange("p c t -> p (c t)"),
+            )
+
+        qT = []
+        kT = []
+
+        def turn_q(h):
+            qT_ps = psum_prep.tile([P, S], BF16, tag="prep")
+            for t in range(TOKEN_TILES):
+                nc.tensor.transpose(
+                    qT_ps[:, t * P : (t + 1) * P], q_sb[h][:, t, :], ident_bf[:]
+                )
+            qT_h = const.tile([P, S], BF16, name="qT%d" % h)
+            nc.scalar.copy(out=qT_h[:], in_=qT_ps[:])
+            qT.append(qT_h)
+
+        def turn_k(h):
+            kT_ps = psum_prep.tile([P, S], BF16, tag="prep")
+            for t in range(TOKEN_TILES):
+                nc.tensor.transpose(
+                    kT_ps[:, t * P : (t + 1) * P], k_sb[h][:, t, :], ident_kept[:, t, :]
+                )
+            kT_h = const.tile([P, S], BF16, name="kT%d" % h)
+            nc.scalar.copy(out=kT_h[:], in_=kT_ps[:])
+            kT.append(kT_h)
+
+        s_ps = {}
+        neg_max = {}
+        e_bf = {}
+        row_sum = {}
+        eT_ps = {}
+        e_grouped = {}
+        e_codes = {}
+        e_scales = {}
+        inv_sum = {}
+        acc = {}
+
+        def scores(n):
+            h, t = divmod(n, TOKEN_TILES)
+            s_ps[n] = psum_s.tile([P, S], F32, name="s_ps")
+            nc.tensor.matmul(
+                s_ps[n][:], lhsT=qT[h][:, t * P : (t + 1) * P], rhs=kT[h][:],
+                start=True, stop=False,
+            )
+            for kt in range(TOKEN_TILES):
+                nc.tensor.matmul(
+                    s_ps[n][:, kt * P : (kt + 1) * P],
+                    lhsT=mask_cols[:, kt, :], rhs=ident_f32[:], is_transpose=True,
+                    start=False, stop=(kt == TOKEN_TILES - 1),
+                )
+
+        def row_maximum(n):
+            scaled = work.tile([P, S], BF16, name="scaled")
+            neg_max[n] = small.tile([P, 1], F32, name="neg_max")
+            nc.vector.tensor_scalar(
+                out=scaled[:], in0=s_ps[n][:], scalar1=-SCALE, scalar2=None,
+                op0=ALU.mult, op1=ALU.min, accum_out=neg_max[n][:],
+            )
+
+        def exponential(n):
+            e_bf[n] = work.tile([P, S], BF16, name="e_bf")
+            row_sum[n] = small.tile([P, 1], F32, name="row_sum")
+            nc.scalar.activation(
+                out=e_bf[n][:].rearrange("q (u p e) -> q u p e", u=2, e=2),
+                in_=s_ps[n][:].rearrange("q (p u e) -> q u p e", u=2, e=2),
+                func=ACT.Exp,
+                bias=neg_max[n][:], scale=SCALE, accum_out=row_sum[n][:],
+            )
+
+        def turn_e(n):
+            eT_ps[n] = psum_eT.tile([P, 2, P], F32, name="eT_ps")
+            e_words = e_bf[n][:].bitcast(F32)
+            for u in range(2):
+                nc.tensor.transpose(
+                    eT_ps[n][:, u, :], e_words[:, u * P : (u + 1) * P], ident_f32[:]
+                )
+
+        def group_e(n):
+            e_grouped[n] = work.tile([P, P * PACK], BF16, name="e_grouped", align_bytes=64)
+            nc.scalar.copy(
+                out=e_grouped[n][:].bitcast(F32).rearrange("p (q u) -> p q u", u=2),
+                in_=eT_ps[n][:].rearrange("p u q -> p q u"),
+            )
+
+        def quantise_e(n):
+            e_codes[n] = work.tile([P, P], U32, name="e_codes", align_bytes=64)
+            e_scales[n] = work.tile([P, P], U8, name="e_scales", align_bytes=64)
+            nc.vector.quantize_mx(
+                out=e_codes[n][:].bitcast(FP8X4), scales=e_scales[n][:],
+                in_=e_grouped[n][:],
+            )
+            inv_sum[n] = small.tile([P, 1], F32, name="inv_sum")
+            nc.vector.reciprocal(out=inv_sum[n][:], in_=row_sum[n][:])
+
+        def attend(n):
+            h = n // TOKEN_TILES
+            head_cols = slice(h * HD, (h + 1) * HD)
+            acc[n] = psum_acc.tile([P, HD], F32, name="acc", tag="acc")
+            nc.tensor.matmul_mx(
+                out=acc[n][:],
+                lhsT=e_codes[n][:].bitcast(FP8X4), lhsT_scale=e_scales[n][:],
+                rhs=v_codes[:, head_cols].bitcast(FP8X4), rhs_scale=v_scales[:, head_cols],
+                start=True, stop=True,
+            )
+
+        def divide_and_store(n):
+            h, t = divmod(n, TOKEN_TILES)
+            o_sb = work.tile([P, HD], F32, name="o_sb")
+            nc.vector.tensor_scalar_mul(out=o_sb[:], in0=acc[n][:], scalar1=inv_sum[n][:])
+            nc.sync.dma_start(out=out_dram[:, t, h * HD : (h + 1) * HD], in_=o_sb[:])
+
+        def in_range(n):
+            return 0 <= n < TILES
+
+        def pipeline_round(r):
+            if in_range(r - 6):
+                attend(r - 6)
+            if in_range(r):
+                scores(r)
+            if in_range(r - 1):
+                row_maximum(r - 1)
+            if in_range(r - 2):
+                exponential(r - 2)
+            if in_range(r - 3):
+                turn_e(r - 3)
+            if in_range(r - 4):
+                group_e(r - 4)
+            if in_range(r - 7):
+                divide_and_store(r - 7)
+            if in_range(r - 5):
+                quantise_e(r - 5)
+            next_head = r // TOKEN_TILES + 1
+            if next_head < HEADS:
+                if r % TOKEN_TILES == 1:
+                    turn_q(next_head)
+                if r % TOKEN_TILES == 2:
+                    turn_k(next_head)
+
+        turn_q(0)
+        turn_k(0)
+        for r in range(TILES + 8):
+            pipeline_round(r)
+            if r == V_ROUND:
+                quantise_v()

@@ -19,7 +19,7 @@ TOKEN_TILES = S // P
 TILES = HEADS * TOKEN_TILES
 PACK = 4
 SCALE = 1.0 / math.sqrt(HD)
-V_ROUND = 2
+V_ROUND = 1
 
 FLOPS = 2 * (2 * HEADS * S * S * HD)
 
@@ -44,20 +44,21 @@ def tile_knnattention_s_kernel(
         tc.manual_schedule(),
     ):
         mask_row = const.tile([P, S], BF16)
-        nc.gpsimd.memset(mask_row[:].bitcast(F32), 0.0)
+        nc.vector.memset(mask_row[:].bitcast(F32), 0.0)
         nc.sync.dma_start(out=mask_row[0:1, :], in_=attention_mask)
         q_sb = []
         k_sb = []
         v_raw = const.tile([P, PACK, S], BF16)
-        for h in range(HEADS):
-            head_cols = slice(h * HD, (h + 1) * HD)
-            q_h = const.tile([P, TOKEN_TILES, HD], BF16, name="q_sb%d" % h)
-            nc.sync.dma_start(out=q_h[:], in_=q_dram[:, :, head_cols])
-            q_sb.append(q_h)
-            k_h = const.tile([P, TOKEN_TILES, HD], BF16, name="k_sb%d" % h)
-            nc.sync.dma_start(out=k_h[:], in_=k_dram[:, :, head_cols])
-            k_sb.append(k_h)
-            if h == 0:
+        for pair in range(HEADS // 2):
+            pair_cols = slice(2 * pair * HD, 2 * (pair + 1) * HD)
+            q_2 = const.tile([P, TOKEN_TILES, 2 * HD], BF16, name="q_sb%d" % pair)
+            nc.sync.dma_start(out=q_2[:], in_=q_dram[:, :, pair_cols])
+            k_2 = const.tile([P, TOKEN_TILES, 2 * HD], BF16, name="k_sb%d" % pair)
+            nc.sync.dma_start(out=k_2[:], in_=k_dram[:, :, pair_cols])
+            for half in range(2):
+                q_sb.append(q_2[:, :, half * HD : (half + 1) * HD])
+                k_sb.append(k_2[:, :, half * HD : (half + 1) * HD])
+            if pair == 0:
                 nc.sync.dma_start(
                     out=v_raw[:].rearrange("p j c -> p (j c)"), in_=v_dram
                 )
@@ -72,36 +73,47 @@ def tile_knnattention_s_kernel(
         nc.vector.memset(warm[:], 0.0)
         nc.scalar.activation(out=warm[:], in_=warm[:], func=ACT.Exp)
 
-        mask_ps = psum_acc.tile([P, TOKEN_TILES, P], F32, tag="acc")
+        mask_ps = psum_acc.tile([P, TOKEN_TILES, 2], F32, tag="acc")
         for t in range(TOKEN_TILES):
             nc.tensor.matmul(
-                mask_ps[:, t, :], lhsT=mask_row[:, t * P : (t + 1) * P], rhs=ones[:],
+                mask_ps[:, t, :], lhsT=mask_row[:, t * P : (t + 1) * P], rhs=ones[:, 0:2],
                 start=True, stop=True,
             )
-        ident_kept = const.tile([P, TOKEN_TILES, P], BF16)
-        nc.vector.scalar_tensor_tensor(
-            out=ident_kept[:],
-            in0=mask_ps[:],
-            scalar=0.0,
-            in1=ident_bf[:].unsqueeze(1).to_broadcast([P, TOKEN_TILES, P]),
-            op0=ALU.is_equal,
-            op1=ALU.mult,
+        kept = const.tile([P, TOKEN_TILES, 2], F32)
+        nc.vector.tensor_scalar(
+            out=kept[:], in0=mask_ps[:], scalar1=0.0, scalar2=None, op0=ALU.is_equal
         )
+        mask_add = const.tile([P, TOKEN_TILES, 2], F32)
+        nc.vector.tensor_scalar_mul(out=mask_add[:], in0=mask_ps[:], scalar1=math.sqrt(HD))
+        ident_kept = const.tile([P, TOKEN_TILES, P], BF16)
+        for t in range(TOKEN_TILES):
+            nc.vector.tensor_scalar_mul(
+                out=ident_kept[:, t, :], in0=ident_bf[:], scalar1=kept[:, t, 0:1]
+            )
         mask_cols = const.tile([P, TOKEN_TILES, P], F32)
-        nc.vector.tensor_scalar_mul(out=mask_cols[:], in0=mask_ps[:], scalar1=math.sqrt(HD))
+
+        def spread_mask():
+            nc.vector.tensor_copy(
+                out=mask_cols[:], in_=mask_add[:, :, 0:1].to_broadcast([P, TOKEN_TILES, P])
+            )
 
         v_grouped = const.tile([P, S, PACK], BF16, align_bytes=64)
         v_codes = const.tile([P, S], U32, align_bytes=64)
         v_scales = const.tile([P, S], U8, align_bytes=64)
 
-        def quantise_v():
+        def group_v(h):
+            head_cols = slice(h * HD, (h + 1) * HD)
             nc.vector.tensor_copy(
-                out=v_grouped[:], in_=v_raw[:].rearrange("p t c -> p c t")
+                out=v_grouped[:, head_cols, :],
+                in_=v_raw[:, :, head_cols].rearrange("p t c -> p c t"),
             )
+
+        def quantise_v(h):
+            head_cols = slice(h * HD, (h + 1) * HD)
             nc.vector.quantize_mx(
-                out=v_codes[:].bitcast(FP8X4),
-                scales=v_scales[:],
-                in_=v_grouped[:].rearrange("p c t -> p (c t)"),
+                out=v_codes[:, head_cols].bitcast(FP8X4),
+                scales=v_scales[:, head_cols],
+                in_=v_grouped[:, head_cols, :].rearrange("p c t -> p (c t)"),
             )
 
         qT = []
@@ -114,17 +126,23 @@ def tile_knnattention_s_kernel(
                     qT_ps[:, t * P : (t + 1) * P], q_sb[h][:, t, :], ident_bf[:]
                 )
             qT_h = const.tile([P, S], BF16, name="qT%d" % h)
-            nc.scalar.copy(out=qT_h[:], in_=qT_ps[:])
+            nc.scalar.copy(out=qT_h[:].bitcast(F32), in_=qT_ps[:].bitcast(F32))
             qT.append(qT_h)
 
         def turn_k(h):
-            kT_ps = psum_prep.tile([P, S], BF16, tag="prep")
+            if h == 0:
+                kT_ps = psum_eT.tile([P, S], BF16, name="eT_ps")
+            else:
+                kT_ps = psum_prep.tile([P, S], BF16, tag="prep")
             for t in range(TOKEN_TILES):
                 nc.tensor.transpose(
                     kT_ps[:, t * P : (t + 1) * P], k_sb[h][:, t, :], ident_kept[:, t, :]
                 )
             kT_h = const.tile([P, S], BF16, name="kT%d" % h)
-            nc.scalar.copy(out=kT_h[:], in_=kT_ps[:])
+            if h == 0:
+                nc.vector.tensor_copy(out=kT_h[:].bitcast(F32), in_=kT_ps[:].bitcast(F32))
+            else:
+                nc.scalar.copy(out=kT_h[:].bitcast(F32), in_=kT_ps[:].bitcast(F32))
             kT.append(kT_h)
 
         s_ps = {}
@@ -241,7 +259,12 @@ def tile_knnattention_s_kernel(
 
         turn_q(0)
         turn_k(0)
+        spread_mask()
         for r in range(TILES + 8):
             pipeline_round(r)
-            if r == V_ROUND:
-                quantise_v()
+            head, phase = divmod(r - V_ROUND, TOKEN_TILES)
+            if 0 <= head < HEADS:
+                if phase == 0:
+                    group_v(head)
+                if phase == 1:
+                    quantise_v(head)

@@ -19,7 +19,6 @@ TOKEN_TILES = S // P
 TILES = HEADS * TOKEN_TILES
 PACK = 4
 SCALE = 1.0 / math.sqrt(HD)
-V_ROUND = 1
 
 FLOPS = 2 * (2 * HEADS * S * S * HD)
 
@@ -37,75 +36,118 @@ def tile_knnattention_s_kernel(
         tc.tile_pool(name="const", bufs=1) as const,
         tc.tile_pool(name="work", bufs=4) as work,
         tc.tile_pool(name="small", bufs=8) as small,
-        tc.psum_pool(name="psum_prep", bufs=1) as psum_prep,
-        tc.psum_pool(name="psum_s", bufs=3) as psum_s,
+        tc.psum_pool(name="psum_s", bufs=4) as psum_s,
         tc.psum_pool(name="psum_eT", bufs=2) as psum_eT,
         tc.psum_pool(name="psum_acc", bufs=2) as psum_acc,
         tc.manual_schedule(),
     ):
-        mask_row = const.tile([P, S], BF16)
-        nc.vector.memset(mask_row[:].bitcast(F32), 0.0)
-        nc.sync.dma_start(out=mask_row[0:1, :], in_=attention_mask)
-        q_sb = []
-        k_sb = []
+        mask_rows = const.tile([P, P], BF16)
+        nc.vector.memset(mask_rows[:].bitcast(F32), 0.0)
+        q_first = const.tile([P, TOKEN_TILES, HD], BF16)
+        k_first = const.tile([P, TOKEN_TILES, HD], BF16)
+        q_rest = const.tile([P, TOKEN_TILES, S - HD], BF16)
+        k_rest = const.tile([P, TOKEN_TILES, S - HD], BF16)
         v_raw = const.tile([P, PACK, S], BF16)
-        for pair in range(HEADS // 2):
-            pair_cols = slice(2 * pair * HD, 2 * (pair + 1) * HD)
-            q_2 = const.tile([P, TOKEN_TILES, 2 * HD], BF16, name="q_sb%d" % pair)
-            nc.sync.dma_start(out=q_2[:], in_=q_dram[:, :, pair_cols])
-            k_2 = const.tile([P, TOKEN_TILES, 2 * HD], BF16, name="k_sb%d" % pair)
-            nc.sync.dma_start(out=k_2[:], in_=k_dram[:, :, pair_cols])
-            for half in range(2):
-                q_sb.append(q_2[:, :, half * HD : (half + 1) * HD])
-                k_sb.append(k_2[:, :, half * HD : (half + 1) * HD])
-            if pair == 0:
-                nc.sync.dma_start(
-                    out=v_raw[:].rearrange("p j c -> p (j c)"), in_=v_dram
-                )
+        nc.sync.dma_start(
+            out=mask_rows[0:TOKEN_TILES, :],
+            in_=attention_mask.rearrange("o (t p) -> (o t) p", p=P),
+        )
+        nc.sync.dma_start(out=q_first[:], in_=q_dram[:, :, 0:HD])
+        nc.sync.dma_start(out=k_first[:], in_=k_dram[:, :, 0:HD])
+        nc.sync.dma_start(out=v_raw[:].rearrange("p j c -> p (j c)"), in_=v_dram)
+        nc.sync.dma_start(out=k_rest[:], in_=k_dram[:, :, HD:S])
+        nc.sync.dma_start(out=q_rest[:], in_=q_dram[:, :, HD:S])
+
+        def q_sb(h, t):
+            if h == 0:
+                return q_first[:, t, :]
+            return q_rest[:, t, (h - 1) * HD : h * HD]
+
+        def k_sb(h, t):
+            if h == 0:
+                return k_first[:, t, :]
+            return k_rest[:, t, (h - 1) * HD : h * HD]
 
         ident_bf = const.tile([P, P], BF16)
         make_identity(nc, ident_bf[:])
         ident_f32 = const.tile([P, P], F32)
         make_identity(nc, ident_f32[:])
-        ones = const.tile([P, P], BF16)
-        nc.vector.memset(ones[:], 1.0)
         warm = const.tile([P, 1], F32)
         nc.vector.memset(warm[:], 0.0)
         nc.scalar.activation(out=warm[:], in_=warm[:], func=ACT.Exp)
 
-        mask_ps = psum_acc.tile([P, TOKEN_TILES, 2], F32, tag="acc")
-        for t in range(TOKEN_TILES):
-            nc.tensor.matmul(
-                mask_ps[:, t, :], lhsT=mask_row[:, t * P : (t + 1) * P], rhs=ones[:, 0:2],
-                start=True, stop=True,
-            )
-        kept = const.tile([P, TOKEN_TILES, 2], F32)
+        mask_ps = psum_acc.tile([P, P], BF16, name="acc")
+        nc.tensor.transpose(mask_ps[:], mask_rows[:], ident_bf[:])
+        mask_by_key = mask_ps[:, 0:TOKEN_TILES]
+        kept = const.tile([P, TOKEN_TILES], F32)
         nc.vector.tensor_scalar(
-            out=kept[:], in0=mask_ps[:], scalar1=0.0, scalar2=None, op0=ALU.is_equal
+            out=kept[:], in0=mask_by_key, scalar1=0.0, scalar2=None, op0=ALU.is_equal
         )
-        mask_add = const.tile([P, TOKEN_TILES, 2], F32)
-        nc.vector.tensor_scalar_mul(out=mask_add[:], in0=mask_ps[:], scalar1=math.sqrt(HD))
+        mask_add = const.tile([P, TOKEN_TILES], F32)
+        nc.vector.tensor_scalar_mul(out=mask_add[:], in0=mask_by_key, scalar1=math.sqrt(HD))
         ident_kept = const.tile([P, TOKEN_TILES, P], BF16)
         for t in range(TOKEN_TILES):
             nc.vector.tensor_scalar_mul(
-                out=ident_kept[:, t, :], in0=ident_bf[:], scalar1=kept[:, t, 0:1]
+                out=ident_kept[:, t, :], in0=ident_bf[:], scalar1=kept[:, t : t + 1]
             )
         mask_cols = const.tile([P, TOKEN_TILES, P], F32)
+        nc.vector.tensor_copy(
+            out=mask_cols[:], in_=mask_add[:].unsqueeze(2).to_broadcast([P, TOKEN_TILES, P])
+        )
 
-        def spread_mask():
-            nc.vector.tensor_copy(
-                out=mask_cols[:], in_=mask_add[:, :, 0:1].to_broadcast([P, TOKEN_TILES, P])
+        qT = {}
+        kT = {}
+        qT_ps = psum_acc.tile([P, S], BF16, name="acc")
+        for t in range(TOKEN_TILES):
+            nc.tensor.transpose(qT_ps[:, t * P : (t + 1) * P], q_sb(0, t), ident_bf[:])
+        qT_first = const.tile([P, S], BF16)
+        nc.scalar.copy(out=qT_first[:].bitcast(F32), in_=qT_ps[:].bitcast(F32))
+        qT[0] = qT_first[:]
+
+        kT_first = const.tile([P, S], BF16)
+        for half, copy in enumerate((nc.scalar.copy, nc.vector.tensor_copy)):
+            kT_ps = psum_eT.tile([P, S // 2], BF16, name="eT_ps")
+            for i in range(TOKEN_TILES // 2):
+                t = half * TOKEN_TILES // 2 + i
+                nc.tensor.transpose(
+                    kT_ps[:, i * P : (i + 1) * P], k_sb(0, t), ident_kept[:, t, :]
+                )
+            keys = slice(half * S // 2, (half + 1) * S // 2)
+            copy(out=kT_first[:, keys].bitcast(F32), in_=kT_ps[:].bitcast(F32))
+        kT[0] = kT_first[:]
+
+        turned_ps = {}
+
+        def turn_head(h):
+            turned_ps[h] = psum_acc.tile([P, 2, S], BF16, name="acc")
+            for t in range(TOKEN_TILES):
+                nc.tensor.transpose(
+                    turned_ps[h][:, 0, t * P : (t + 1) * P], q_sb(h, t), ident_bf[:]
+                )
+            for t in range(TOKEN_TILES):
+                nc.tensor.transpose(
+                    turned_ps[h][:, 1, t * P : (t + 1) * P], k_sb(h, t), ident_kept[:, t, :]
+                )
+
+        def copy_head(h):
+            turned = const.tile([P, 2, S], BF16, name="turned%d" % h)
+            nc.scalar.copy(
+                out=turned[:].rearrange("p a s -> p (a s)").bitcast(F32),
+                in_=turned_ps[h][:].rearrange("p a s -> p (a s)").bitcast(F32),
             )
+            qT[h] = turned[:, 0, :]
+            kT[h] = turned[:, 1, :]
 
         v_grouped = const.tile([P, S, PACK], BF16, align_bytes=64)
         v_codes = const.tile([P, S], U32, align_bytes=64)
         v_scales = const.tile([P, S], U8, align_bytes=64)
 
-        def group_v(h):
+        for h in range(HEADS):
             head_cols = slice(h * HD, (h + 1) * HD)
-            nc.vector.tensor_copy(
+            nc.gpsimd.tensor_scalar(
                 out=v_grouped[:, head_cols, :],
-                in_=v_raw[:, :, head_cols].rearrange("p t c -> p c t"),
+                in0=v_raw[:, :, head_cols].rearrange("p t c -> p c t"),
+                scalar1=1.0, scalar2=0.0, op0=ALU.mult, op1=ALU.add,
             )
 
         def quantise_v(h):
@@ -116,39 +158,56 @@ def tile_knnattention_s_kernel(
                 in_=v_grouped[:, head_cols, :].rearrange("p c t -> p (c t)"),
             )
 
-        qT = []
-        kT = []
-
-        def turn_q(h):
-            qT_ps = psum_prep.tile([P, S], BF16, tag="prep")
-            for t in range(TOKEN_TILES):
-                nc.tensor.transpose(
-                    qT_ps[:, t * P : (t + 1) * P], q_sb[h][:, t, :], ident_bf[:]
-                )
-            qT_h = const.tile([P, S], BF16, name="qT%d" % h)
-            nc.scalar.copy(out=qT_h[:].bitcast(F32), in_=qT_ps[:].bitcast(F32))
-            qT.append(qT_h)
-
-        def turn_k(h):
-            if h == 0:
-                kT_ps = psum_eT.tile([P, S], BF16, name="eT_ps")
-            else:
-                kT_ps = psum_prep.tile([P, S], BF16, tag="prep")
-            for t in range(TOKEN_TILES):
-                nc.tensor.transpose(
-                    kT_ps[:, t * P : (t + 1) * P], k_sb[h][:, t, :], ident_kept[:, t, :]
-                )
-            kT_h = const.tile([P, S], BF16, name="kT%d" % h)
-            if h == 0:
-                nc.vector.tensor_copy(out=kT_h[:].bitcast(F32), in_=kT_ps[:].bitcast(F32))
-            else:
-                nc.scalar.copy(out=kT_h[:].bitcast(F32), in_=kT_ps[:].bitcast(F32))
-            kT.append(kT_h)
-
         s_ps = {}
         neg_max = {}
         e_bf = {}
         row_sum = {}
+
+        def open_scores(n):
+            s_ps[n] = psum_s.tile([P, S], F32, name="s_ps")
+
+        def multiply(n, first):
+            h, t = divmod(n, TOKEN_TILES)
+            nc.tensor.matmul(
+                s_ps[n][:], lhsT=qT[h][:, t * P : (t + 1) * P], rhs=kT[h],
+                start=first, stop=not first,
+            )
+
+        def lay_mask(n, first):
+            for kt in range(TOKEN_TILES):
+                nc.tensor.matmul(
+                    s_ps[n][:, kt * P : (kt + 1) * P],
+                    lhsT=mask_cols[:, kt, :], rhs=ident_f32[:], is_transpose=True,
+                    start=first and kt == 0,
+                    stop=not first and kt == TOKEN_TILES - 1,
+                )
+
+        def scores(n):
+            open_scores(n)
+            multiply(n, first=True)
+            lay_mask(n, first=False)
+
+        def row_maximum(n):
+            neg_max[n] = small.tile([P, 1], F32, name="neg_max")
+            scaled = work.tile([P, S], BF16, name="scaled")
+            nc.vector.tensor_scalar(
+                out=scaled[:], in0=s_ps[n][:], scalar1=-SCALE, scalar2=None,
+                op0=ALU.mult, op1=ALU.min, accum_out=neg_max[n][:],
+            )
+
+        def exponential(n):
+            pair, member = divmod(n, 2)
+            if pair not in row_sum:
+                row_sum[pair] = small.tile([P, 2], F32, name="row_sum")
+            e_bf[n] = work.tile([P, S], BF16, name="e_bf")
+            nc.scalar.activation(
+                out=e_bf[n][:].rearrange("q (u p e) -> q u p e", u=2, e=2),
+                in_=s_ps[n][:].rearrange("q (p u e) -> q u p e", u=2, e=2),
+                func=ACT.Exp,
+                bias=neg_max[n][:], scale=SCALE,
+                accum_out=row_sum[pair][:, member : member + 1],
+            )
+
         eT_ps = {}
         e_grouped = {}
         e_codes = {}
@@ -156,115 +215,116 @@ def tile_knnattention_s_kernel(
         inv_sum = {}
         acc = {}
 
-        def scores(n):
-            h, t = divmod(n, TOKEN_TILES)
-            s_ps[n] = psum_s.tile([P, S], F32, name="s_ps")
-            nc.tensor.matmul(
-                s_ps[n][:], lhsT=qT[h][:, t * P : (t + 1) * P], rhs=kT[h][:],
-                start=True, stop=False,
+        def turn_e(unit):
+            first, count = unit
+            eT_ps[unit] = psum_eT.tile([P, count, 2, P], F32, name="eT_ps")
+            for i in range(count):
+                e_words = e_bf[first + i][:].bitcast(F32)
+                for u in range(2):
+                    nc.tensor.transpose(
+                        eT_ps[unit][:, i, u, :], e_words[:, u * P : (u + 1) * P], ident_f32[:]
+                    )
+
+        def group_e(unit):
+            first, count = unit
+            e_grouped[unit] = work.tile(
+                [P, count * P * PACK], BF16, name="e_grouped", align_bytes=64
             )
-            for kt in range(TOKEN_TILES):
-                nc.tensor.matmul(
-                    s_ps[n][:, kt * P : (kt + 1) * P],
-                    lhsT=mask_cols[:, kt, :], rhs=ident_f32[:], is_transpose=True,
-                    start=False, stop=(kt == TOKEN_TILES - 1),
-                )
-
-        def row_maximum(n):
-            scaled = work.tile([P, S], BF16, name="scaled")
-            neg_max[n] = small.tile([P, 1], F32, name="neg_max")
-            nc.vector.tensor_scalar(
-                out=scaled[:], in0=s_ps[n][:], scalar1=-SCALE, scalar2=None,
-                op0=ALU.mult, op1=ALU.min, accum_out=neg_max[n][:],
-            )
-
-        def exponential(n):
-            e_bf[n] = work.tile([P, S], BF16, name="e_bf")
-            row_sum[n] = small.tile([P, 1], F32, name="row_sum")
-            nc.scalar.activation(
-                out=e_bf[n][:].rearrange("q (u p e) -> q u p e", u=2, e=2),
-                in_=s_ps[n][:].rearrange("q (p u e) -> q u p e", u=2, e=2),
-                func=ACT.Exp,
-                bias=neg_max[n][:], scale=SCALE, accum_out=row_sum[n][:],
-            )
-
-        def turn_e(n):
-            eT_ps[n] = psum_eT.tile([P, 2, P], F32, name="eT_ps")
-            e_words = e_bf[n][:].bitcast(F32)
-            for u in range(2):
-                nc.tensor.transpose(
-                    eT_ps[n][:, u, :], e_words[:, u * P : (u + 1) * P], ident_f32[:]
-                )
-
-        def group_e(n):
-            e_grouped[n] = work.tile([P, P * PACK], BF16, name="e_grouped", align_bytes=64)
             nc.scalar.copy(
-                out=e_grouped[n][:].bitcast(F32).rearrange("p (q u) -> p q u", u=2),
-                in_=eT_ps[n][:].rearrange("p u q -> p q u"),
+                out=e_grouped[unit][:].bitcast(F32).rearrange(
+                    "p (i q u) -> p i q u", i=count, u=2
+                ),
+                in_=eT_ps[unit][:].rearrange("p i u q -> p i q u"),
             )
 
-        def quantise_e(n):
-            e_codes[n] = work.tile([P, P], U32, name="e_codes", align_bytes=64)
-            e_scales[n] = work.tile([P, P], U8, name="e_scales", align_bytes=64)
+        def quantise_e(unit):
+            first, count = unit
+            pair, member = divmod(first, 2)
+            e_codes[unit] = work.tile([P, count * P], U32, name="e_codes", align_bytes=64)
+            e_scales[unit] = work.tile([P, count * P], U8, name="e_scales", align_bytes=64)
             nc.vector.quantize_mx(
-                out=e_codes[n][:].bitcast(FP8X4), scales=e_scales[n][:],
-                in_=e_grouped[n][:],
+                out=e_codes[unit][:].bitcast(FP8X4), scales=e_scales[unit][:],
+                in_=e_grouped[unit][:],
             )
-            inv_sum[n] = small.tile([P, 1], F32, name="inv_sum")
-            nc.vector.reciprocal(out=inv_sum[n][:], in_=row_sum[n][:])
+            inv_sum[unit] = small.tile([P, count], F32, name="inv_sum")
+            nc.vector.reciprocal(
+                out=inv_sum[unit][:], in_=row_sum[pair][:, member : member + count]
+            )
 
-        def attend(n):
-            h = n // TOKEN_TILES
+        def attend(unit):
+            first, count = unit
+            h = first // TOKEN_TILES
             head_cols = slice(h * HD, (h + 1) * HD)
-            acc[n] = psum_acc.tile([P, HD], F32, name="acc", tag="acc")
-            nc.tensor.matmul_mx(
-                out=acc[n][:],
-                lhsT=e_codes[n][:].bitcast(FP8X4), lhsT_scale=e_scales[n][:],
-                rhs=v_codes[:, head_cols].bitcast(FP8X4), rhs_scale=v_scales[:, head_cols],
-                start=True, stop=True,
+            if count == 1:
+                acc[unit] = psum_s.tile([P, count, HD], F32, name="s_ps")
+            else:
+                acc[unit] = psum_acc.tile([P, count, HD], F32, name="acc")
+            for i in range(count):
+                queries = slice(i * P, (i + 1) * P)
+                nc.tensor.matmul_mx(
+                    out=acc[unit][:, i, :],
+                    lhsT=e_codes[unit][:, queries].bitcast(FP8X4),
+                    lhsT_scale=e_scales[unit][:, queries],
+                    rhs=v_codes[:, head_cols].bitcast(FP8X4), rhs_scale=v_scales[:, head_cols],
+                    start=True, stop=True,
+                )
+
+        def divide_and_store(unit):
+            first, count = unit
+            h, t = divmod(first, TOKEN_TILES)
+            o_sb = work.tile([P, count, HD], F32, name="o_sb")
+            nc.vector.tensor_mul(
+                out=o_sb[:], in0=acc[unit][:],
+                in1=inv_sum[unit][:].unsqueeze(2).to_broadcast([P, count, HD]),
+            )
+            nc.sync.dma_start(
+                out=out_dram[:, t : t + count, h * HD : (h + 1) * HD], in_=o_sb[:]
             )
 
-        def divide_and_store(n):
-            h, t = divmod(n, TOKEN_TILES)
-            o_sb = work.tile([P, HD], F32, name="o_sb")
-            nc.vector.tensor_scalar_mul(out=o_sb[:], in0=acc[n][:], scalar1=inv_sum[n][:])
-            nc.sync.dma_start(out=out_dram[:, t, h * HD : (h + 1) * HD], in_=o_sb[:])
+        LAG = {
+            "maximum": 1, "exponential": 2, "turn": 3, "group": 4, "quantise": 6,
+            "attend": 8, "divide": 9,
+        }
 
-        def in_range(n):
-            return 0 <= n < TILES
+        def units_at(n):
+            if n in (TILES - 2, TILES - 1):
+                return [(n, 1)]
+            if 0 <= n < TILES and n % 2 == 1:
+                return [(n - 1, 2)]
+            return []
+
+        def tiles_at(n):
+            return [n] if 0 <= n < TILES else []
 
         def pipeline_round(r):
-            if in_range(r - 6):
-                attend(r - 6)
-            if in_range(r):
-                scores(r)
-            if in_range(r - 1):
-                row_maximum(r - 1)
-            if in_range(r - 2):
-                exponential(r - 2)
-            if in_range(r - 3):
-                turn_e(r - 3)
-            if in_range(r - 4):
-                group_e(r - 4)
-            if in_range(r - 7):
-                divide_and_store(r - 7)
-            if in_range(r - 5):
-                quantise_e(r - 5)
+            for unit in units_at(r - LAG["attend"]):
+                attend(unit)
+            for n in tiles_at(r):
+                if n == 0:
+                    multiply(n, first=False)
+                else:
+                    scores(n)
+            for unit in units_at(r - LAG["turn"]):
+                turn_e(unit)
+            for n in tiles_at(r - LAG["maximum"]):
+                row_maximum(n)
+            for unit in units_at(r - LAG["quantise"]):
+                quantise_e(unit)
+            for unit in units_at(r - LAG["divide"]):
+                divide_and_store(unit)
+            for n in tiles_at(r - LAG["exponential"]):
+                exponential(n)
+            for unit in units_at(r - LAG["group"]):
+                group_e(unit)
             next_head = r // TOKEN_TILES + 1
-            if next_head < HEADS:
-                if r % TOKEN_TILES == 1:
-                    turn_q(next_head)
-                if r % TOKEN_TILES == 2:
-                    turn_k(next_head)
+            if r % TOKEN_TILES == 2 and next_head < HEADS:
+                turn_head(next_head)
+                copy_head(next_head)
+            head, phase = divmod(r, TOKEN_TILES)
+            if phase == 2 and head < HEADS:
+                quantise_v(head)
 
-        turn_q(0)
-        turn_k(0)
-        spread_mask()
-        for r in range(TILES + 8):
+        open_scores(0)
+        lay_mask(0, first=True)
+        for r in range(TILES + LAG["divide"]):
             pipeline_round(r)
-            head, phase = divmod(r - V_ROUND, TOKEN_TILES)
-            if 0 <= head < HEADS:
-                if phase == 0:
-                    group_v(head)
-                if phase == 1:
-                    quantise_v(head)

@@ -52,11 +52,12 @@ def tile_knnattention_s_kernel(
             out=mask_rows[0:TOKEN_TILES, :],
             in_=attention_mask.rearrange("o (t p) -> (o t) p", p=P),
         )
-        nc.sync.dma_start(out=q_first[:], in_=q_dram[:, :, 0:HD])
         nc.sync.dma_start(out=k_first[:], in_=k_dram[:, :, 0:HD])
-        nc.sync.dma_start(out=v_raw[:].rearrange("p j c -> p (j c)"), in_=v_dram)
-        nc.sync.dma_start(out=k_rest[:], in_=k_dram[:, :, HD:S])
+        nc.sync.dma_start(out=q_first[:, 0:1, :], in_=q_dram[:, 0:1, 0:HD])
+        nc.sync.dma_start(out=q_first[:, 1:, :], in_=q_dram[:, 1:, 0:HD])
         nc.sync.dma_start(out=q_rest[:], in_=q_dram[:, :, HD:S])
+        nc.sync.dma_start(out=k_rest[:], in_=k_dram[:, :, HD:S])
+        nc.sync.dma_start(out=v_raw[:].rearrange("p j c -> p (j c)"), in_=v_dram)
 
         def q_sb(h, t):
             if h == 0:
@@ -68,6 +69,16 @@ def tile_knnattention_s_kernel(
                 return k_first[:, t, :]
             return k_rest[:, t, (h - 1) * HD : h * HD]
 
+        idle = const.tile([P, P], F32)
+        nc.vector.memset(idle[:], 0.0)
+
+        def keep_busy(times):
+            busy = psum_s.tile([P, P], F32, name="s_ps")
+            for i in range(times):
+                nc.tensor.matmul(busy[:], lhsT=idle[:], rhs=idle[:], start=True, stop=True)
+
+        keep_busy(3)
+
         ident_bf = const.tile([P, P], BF16)
         make_identity(nc, ident_bf[:])
         ident_f32 = const.tile([P, P], F32)
@@ -78,6 +89,7 @@ def tile_knnattention_s_kernel(
 
         mask_ps = psum_acc.tile([P, P], BF16, name="acc")
         nc.tensor.transpose(mask_ps[:], mask_rows[:], ident_bf[:])
+        keep_busy(1)
         mask_by_key = mask_ps[:, 0:TOKEN_TILES]
         kept = const.tile([P, TOKEN_TILES], F32)
         nc.vector.tensor_scalar(
@@ -97,13 +109,6 @@ def tile_knnattention_s_kernel(
 
         qT = {}
         kT = {}
-        qT_ps = psum_acc.tile([P, S], BF16, name="acc")
-        for t in range(TOKEN_TILES):
-            nc.tensor.transpose(qT_ps[:, t * P : (t + 1) * P], q_sb(0, t), ident_bf[:])
-        qT_first = const.tile([P, S], BF16)
-        nc.scalar.copy(out=qT_first[:].bitcast(F32), in_=qT_ps[:].bitcast(F32))
-        qT[0] = qT_first[:]
-
         kT_first = const.tile([P, S], BF16)
         for half, copy in enumerate((nc.scalar.copy, nc.vector.tensor_copy)):
             kT_ps = psum_eT.tile([P, S // 2], BF16, name="eT_ps")
@@ -115,6 +120,19 @@ def tile_knnattention_s_kernel(
             keys = slice(half * S // 2, (half + 1) * S // 2)
             copy(out=kT_first[:, keys].bitcast(F32), in_=kT_ps[:].bitcast(F32))
         kT[0] = kT_first[:]
+
+        qT_first = const.tile([P, S], BF16)
+        qT[0] = qT_first[:]
+
+        def turn_first_q(tiles):
+            qT_ps = psum_acc.tile([P, len(tiles), P], BF16, name="acc")
+            for i, t in enumerate(tiles):
+                nc.tensor.transpose(qT_ps[:, i, :], q_sb(0, t), ident_bf[:])
+            tokens = slice(tiles[0] * P, (tiles[-1] + 1) * P)
+            nc.scalar.copy(
+                out=qT_first[:, tokens].bitcast(F32),
+                in_=qT_ps[:].rearrange("p t c -> p (t c)").bitcast(F32),
+            )
 
         turned_ps = {}
 
@@ -217,7 +235,10 @@ def tile_knnattention_s_kernel(
 
         def turn_e(unit):
             first, count = unit
-            eT_ps[unit] = psum_eT.tile([P, count, 2, P], F32, name="eT_ps")
+            if count == 1:
+                eT_ps[unit] = psum_s.tile([P, count, 2, P], F32, name="s_ps")
+            else:
+                eT_ps[unit] = psum_eT.tile([P, count, 2, P], F32, name="eT_ps")
             for i in range(count):
                 e_words = e_bf[first + i][:].bitcast(F32)
                 for u in range(2):
@@ -300,9 +321,7 @@ def tile_knnattention_s_kernel(
             for unit in units_at(r - LAG["attend"]):
                 attend(unit)
             for n in tiles_at(r):
-                if n == 0:
-                    multiply(n, first=False)
-                else:
+                if n >= 2:
                     scores(n)
             for unit in units_at(r - LAG["turn"]):
                 turn_e(unit)
@@ -320,11 +339,14 @@ def tile_knnattention_s_kernel(
             if r % TOKEN_TILES == 2 and next_head < HEADS:
                 turn_head(next_head)
                 copy_head(next_head)
-            head, phase = divmod(r, TOKEN_TILES)
-            if phase == 2 and head < HEADS:
+            head, phase = divmod(r - 2, TOKEN_TILES)
+            if phase == 2 and 0 <= head < HEADS:
                 quantise_v(head)
 
-        open_scores(0)
-        lay_mask(0, first=True)
+        for n, tiles in ((0, [0]), (1, [1, 2, 3])):
+            turn_first_q(tiles)
+            open_scores(n)
+            lay_mask(n, first=True)
+            multiply(n, first=False)
         for r in range(TILES + LAG["divide"]):
             pipeline_round(r)

@@ -28,7 +28,8 @@ def tile_knnattention_s_kernel(
 ):
     nc = tc.nc
     q_dram = model_hidden_states.flatten_outer_dims().rearrange("(t p) c -> p t c", p=P)
-    k_dram = k_hidden_states.flatten_outer_dims().rearrange("(t p) c -> p t c", p=P)
+    k_dram = k_hidden_states.flatten_outer_dims().rearrange("(p t) c -> p t c", p=P)
+    mask_dram = attention_mask.rearrange("o (p t) -> (o p) t", p=P)
     out_dram = out.flatten_outer_dims().rearrange("(t p) c -> p t c", p=P)
     v_dram = k_embeddings.flatten_outer_dims().rearrange("(p j) c -> p (j c)", j=PACK)
 
@@ -36,22 +37,19 @@ def tile_knnattention_s_kernel(
         tc.tile_pool(name="const", bufs=1) as const,
         tc.tile_pool(name="work", bufs=4) as work,
         tc.tile_pool(name="small", bufs=8) as small,
+        tc.tile_pool(name="results", bufs=TILES // 2 + 1) as results,
         tc.psum_pool(name="psum_s", bufs=4) as psum_s,
         tc.psum_pool(name="psum_eT", bufs=2) as psum_eT,
         tc.psum_pool(name="psum_acc", bufs=2) as psum_acc,
         tc.manual_schedule(),
     ):
-        mask_rows = const.tile([P, P], BF16)
-        nc.vector.memset(mask_rows[:].bitcast(F32), 0.0)
+        mask_by_key = const.tile([P, TOKEN_TILES], BF16)
         q_first = const.tile([P, TOKEN_TILES, HD], BF16)
         k_first = const.tile([P, TOKEN_TILES, HD], BF16)
         q_rest = const.tile([P, TOKEN_TILES, S - HD], BF16)
         k_rest = const.tile([P, TOKEN_TILES, S - HD], BF16)
         v_raw = const.tile([P, PACK, S], BF16)
-        nc.sync.dma_start(
-            out=mask_rows[0:TOKEN_TILES, :],
-            in_=attention_mask.rearrange("o (t p) -> (o t) p", p=P),
-        )
+        nc.sync.dma_start(out=mask_by_key[:], in_=mask_dram)
         nc.sync.dma_start(out=k_first[:], in_=k_dram[:, :, 0:HD])
         nc.sync.dma_start(out=q_first[:, 0:1, :], in_=q_dram[:, 0:1, 0:HD])
         nc.sync.dma_start(out=q_first[:, 1:, :], in_=q_dram[:, 1:, 0:HD])
@@ -87,16 +85,12 @@ def tile_knnattention_s_kernel(
         nc.vector.memset(warm[:], 0.0)
         nc.scalar.activation(out=warm[:], in_=warm[:], func=ACT.Exp)
 
-        mask_ps = psum_acc.tile([P, P], BF16, name="acc")
-        nc.tensor.transpose(mask_ps[:], mask_rows[:], ident_bf[:])
-        keep_busy(1)
-        mask_by_key = mask_ps[:, 0:TOKEN_TILES]
         kept = const.tile([P, TOKEN_TILES], F32)
         nc.vector.tensor_scalar(
-            out=kept[:], in0=mask_by_key, scalar1=0.0, scalar2=None, op0=ALU.is_equal
+            out=kept[:], in0=mask_by_key[:], scalar1=0.0, scalar2=None, op0=ALU.is_equal
         )
         mask_add = const.tile([P, TOKEN_TILES], F32)
-        nc.vector.tensor_scalar_mul(out=mask_add[:], in0=mask_by_key, scalar1=math.sqrt(HD))
+        nc.vector.tensor_scalar_mul(out=mask_add[:], in0=mask_by_key[:], scalar1=math.sqrt(HD))
         ident_kept = const.tile([P, TOKEN_TILES, P], BF16)
         for t in range(TOKEN_TILES):
             nc.vector.tensor_scalar_mul(
@@ -220,7 +214,7 @@ def tile_knnattention_s_kernel(
             e_bf[n] = work.tile([P, S], BF16, name="e_bf")
             nc.scalar.activation(
                 out=e_bf[n][:].rearrange("q (u p e) -> q u p e", u=2, e=2),
-                in_=s_ps[n][:].rearrange("q (p u e) -> q u p e", u=2, e=2),
+                in_=s_ps[n][:].rearrange("q (u e p) -> q u p e", u=2, e=2),
                 func=ACT.Exp,
                 bias=neg_max[n][:], scale=SCALE,
                 accum_out=row_sum[pair][:, member : member + 1],
@@ -293,7 +287,7 @@ def tile_knnattention_s_kernel(
         def divide_and_store(unit):
             first, count = unit
             h, t = divmod(first, TOKEN_TILES)
-            o_sb = work.tile([P, count, HD], F32, name="o_sb")
+            o_sb = results.tile([P, count, HD], F32, name="o_sb")
             nc.vector.tensor_mul(
                 out=o_sb[:], in0=acc[unit][:],
                 in1=inv_sum[unit][:].unsqueeze(2).to_broadcast([P, count, HD]),

import math

import concourse.mybir as mybir
from concourse.masks import make_identity

BF16 = mybir.dt.bfloat16
F32 = mybir.dt.float32
U32 = mybir.dt.uint32
U8 = mybir.dt.uint8
FP8X4 = mybir.dt.float8_e4m3fn_x4
ALU = mybir.AluOpType
ACT = mybir.ActivationFunctionType

P = 128
S = 512
HEADS = 4
HD = 128
TOKEN_TILES = S // P
TILES = HEADS * TOKEN_TILES
PACK = 4
SCALE = 1.0 / math.sqrt(HD)

FLOPS = 2 * (2 * HEADS * S * S * HD)


def tile_knnattention_s_kernel(
    tc, model_hidden_states, k_hidden_states, k_embeddings, attention_mask, out
):
    nc = tc.nc
    q_dram = model_hidden_states.flatten_outer_dims().rearrange("(t p) c -> p t c", p=P)
    k_dram = k_hidden_states.flatten_outer_dims().rearrange("(p t) c -> p t c", p=P)
    mask_dram = attention_mask.rearrange("o (p t) -> (o p) t", p=P)
    out_dram = out.flatten_outer_dims().rearrange("(t p) c -> p t c", p=P)
    v_dram = k_embeddings.flatten_outer_dims().rearrange("(p j) c -> p (j c)", j=PACK)

    with (
        tc.tile_pool(name="const", bufs=1) as const,
        tc.tile_pool(name="work", bufs=4) as work,
        tc.tile_pool(name="small", bufs=8) as small,
        tc.tile_pool(name="results", bufs=TILES // 2 + 1) as results,
        tc.psum_pool(name="psum_s", bufs=4) as psum_s,
        tc.psum_pool(name="psum_eT", bufs=2) as psum_eT,
        tc.psum_pool(name="psum_acc", bufs=2) as psum_acc,
        tc.manual_schedule(),
    ):
        mask_by_key = const.tile([P, TOKEN_TILES], BF16)
        q_first = const.tile([P, TOKEN_TILES, HD], BF16)
        k_first = const.tile([P, TOKEN_TILES, HD], BF16)
        q_rest = const.tile([P, TOKEN_TILES, S - HD], BF16)
        k_rest = const.tile([P, TOKEN_TILES, S - HD], BF16)
        v_raw = const.tile([P, PACK, S], BF16)
        nc.sync.dma_start(out=mask_by_key[:], in_=mask_dram)
        nc.sync.dma_start(out=k_first[:], in_=k_dram[:, :, 0:HD])
        nc.sync.dma_start(out=q_first[:, 0:1, :], in_=q_dram[:, 0:1, 0:HD])
        nc.sync.dma_start(out=q_first[:, 1:, :], in_=q_dram[:, 1:, 0:HD])
        nc.sync.dma_start(out=q_rest[:], in_=q_dram[:, :, HD:S])
        nc.sync.dma_start(out=k_rest[:], in_=k_dram[:, :, HD:S])
        nc.sync.dma_start(out=v_raw[:].rearrange("p j c -> p (j c)"), in_=v_dram)

        def q_sb(h, t):
            if h == 0:
                return q_first[:, t, :]
            return q_rest[:, t, (h - 1) * HD : h * HD]

        def k_sb(h, t):
            if h == 0:
                return k_first[:, t, :]
            return k_rest[:, t, (h - 1) * HD : h * HD]

        idle = const.tile([P, P], F32)
        nc.vector.memset(idle[:], 0.0)

        def keep_busy(times):
            busy = psum_s.tile([P, P], F32, name="s_ps")
            for i in range(times):
                nc.tensor.matmul(busy[:], lhsT=idle[:], rhs=idle[:], start=True, stop=True)

        keep_busy(3)

        ident_bf = const.tile([P, P], BF16)
        make_identity(nc, ident_bf[:])
        ident_f32 = const.tile([P, P], F32)
        make_identity(nc, ident_f32[:])
        warm = const.tile([P, 1], F32)
        nc.vector.memset(warm[:], 0.0)
        nc.scalar.activation(out=warm[:], in_=warm[:], func=ACT.Exp)

        kept = const.tile([P, TOKEN_TILES], F32)
        nc.vector.tensor_scalar(
            out=kept[:], in0=mask_by_key[:], scalar1=0.0, scalar2=None, op0=ALU.is_equal
        )
        mask_add = const.tile([P, TOKEN_TILES], F32)
        nc.vector.tensor_scalar_mul(out=mask_add[:], in0=mask_by_key[:], scalar1=math.sqrt(HD))
        ident_kept = const.tile([P, TOKEN_TILES, P], BF16)
        for t in range(TOKEN_TILES):
            nc.vector.tensor_scalar_mul(
                out=ident_kept[:, t, :], in0=ident_bf[:], scalar1=kept[:, t : t + 1]
            )
        mask_cols = const.tile([P, TOKEN_TILES, P], F32)
        nc.vector.tensor_copy(
            out=mask_cols[:], in_=mask_add[:].unsqueeze(2).to_broadcast([P, TOKEN_TILES, P])
        )

        qT = {}
        kT = {}
        kT_first = const.tile([P, S], BF16)
        for half, copy in enumerate((nc.scalar.copy, nc.vector.tensor_copy)):
            kT_ps = psum_eT.tile([P, S // 2], BF16, name="eT_ps")
            for i in range(TOKEN_TILES // 2):
                t = half * TOKEN_TILES // 2 + i
                nc.tensor.transpose(
                    kT_ps[:, i * P : (i + 1) * P], k_sb(0, t), ident_kept[:, t, :]
                )
            keys = slice(half * S // 2, (half + 1) * S // 2)
            copy(out=kT_first[:, keys].bitcast(F32), in_=kT_ps[:].bitcast(F32))
        kT[0] = kT_first[:]

        qT_first = const.tile([P, S], BF16)
        qT[0] = qT_first[:]

        def turn_first_q(tiles):
            qT_ps = psum_acc.tile([P, len(tiles), P], BF16, name="acc")
            for i, t in enumerate(tiles):
                nc.tensor.transpose(qT_ps[:, i, :], q_sb(0, t), ident_bf[:])
            tokens = slice(tiles[0] * P, (tiles[-1] + 1) * P)
            nc.scalar.copy(
                out=qT_first[:, tokens].bitcast(F32),
                in_=qT_ps[:].rearrange("p t c -> p (t c)").bitcast(F32),
            )

        turned_ps = {}

        def turn_head(h):
            turned_ps[h] = psum_acc.tile([P, 2, S], BF16, name="acc")
            for t in range(TOKEN_TILES):
                nc.tensor.transpose(
                    turned_ps[h][:, 0, t * P : (t + 1) * P], q_sb(h, t), ident_bf[:]
                )
            for t in range(TOKEN_TILES):
                nc.tensor.transpose(
                    turned_ps[h][:, 1, t * P : (t + 1) * P], k_sb(h, t), ident_kept[:, t, :]
                )

        def copy_head(h):
            turned = const.tile([P, 2, S], BF16, name="turned%d" % h)
            nc.scalar.copy(
                out=turned[:].rearrange("p a s -> p (a s)").bitcast(F32),
                in_=turned_ps[h][:].rearrange("p a s -> p (a s)").bitcast(F32),
            )
            qT[h] = turned[:, 0, :]
            kT[h] = turned[:, 1, :]

        v_grouped = const.tile([P, S, PACK], BF16, align_bytes=64)
        v_codes = const.tile([P, S], U32, align_bytes=64)
        v_scales = const.tile([P, S], U8, align_bytes=64)

        for h in range(HEADS):
            head_cols = slice(h * HD, (h + 1) * HD)
            nc.gpsimd.tensor_scalar(
                out=v_grouped[:, head_cols, :],
                in0=v_raw[:, :, head_cols].rearrange("p t c -> p c t"),
                scalar1=1.0, scalar2=0.0, op0=ALU.mult, op1=ALU.add,
            )

        def quantise_v(h):
            head_cols = slice(h * HD, (h + 1) * HD)
            nc.vector.quantize_mx(
                out=v_codes[:, head_cols].bitcast(FP8X4),
                scales=v_scales[:, head_cols],
                in_=v_grouped[:, head_cols, :].rearrange("p c t -> p (c t)"),
            )

        s_ps = {}
        neg_max = {}
        e_bf = {}
        row_sum = {}

        def open_scores(n):
            s_ps[n] = psum_s.tile([P, S], F32, name="s_ps")

        def multiply(n, first):
            h, t = divmod(n, TOKEN_TILES)
            nc.tensor.matmul(
                s_ps[n][:], lhsT=qT[h][:, t * P : (t + 1) * P], rhs=kT[h],
                start=first, stop=not first,
            )

        def lay_mask(n, first):
            for kt in range(TOKEN_TILES):
                nc.tensor.matmul(
                    s_ps[n][:, kt * P : (kt + 1) * P],
                    lhsT=mask_cols[:, kt, :], rhs=ident_f32[:], is_transpose=True,
                    start=first and kt == 0,
                    stop=not first and kt == TOKEN_TILES - 1,
                )

        def scores(n):
            open_scores(n)
            multiply(n, first=True)
            lay_mask(n, first=False)

        def row_maximum(n):
            neg_max[n] = small.tile([P, 1], F32, name="neg_max")
            scaled = work.tile([P, S], BF16, name="scaled")
            nc.vector.tensor_scalar(
                out=scaled[:], in0=s_ps[n][:], scalar1=-SCALE, scalar2=None,
                op0=ALU.mult, op1=ALU.min, accum_out=neg_max[n][:],
            )

        def exponential(n):
            pair, member = divmod(n, 2)
            if pair not in row_sum:
                row_sum[pair] = small.tile([P, 2], F32, name="row_sum")
            e_bf[n] = work.tile([P, S], BF16, name="e_bf")
            nc.scalar.activation(
                out=e_bf[n][:].rearrange("q (u p e) -> q u p e", u=2, e=2),
                in_=s_ps[n][:].rearrange("q (u e p) -> q u p e", u=2, e=2),
                func=ACT.Exp,
                bias=neg_max[n][:], scale=SCALE,
                accum_out=row_sum[pair][:, member : member + 1],
            )

        eT_ps = {}
        e_grouped = {}
        e_codes = {}
        e_scales = {}
        inv_sum = {}
        acc = {}

        def turn_e(unit):
            first, count = unit
            if count == 1:
                eT_ps[unit] = psum_s.tile([P, count, 2, P], F32, name="s_ps")
            else:
                eT_ps[unit] = psum_eT.tile([P, count, 2, P], F32, name="eT_ps")
            for i in range(count):
                e_words = e_bf[first + i][:].bitcast(F32)
                for u in range(2):
                    nc.tensor.transpose(
                        eT_ps[unit][:, i, u, :], e_words[:, u * P : (u + 1) * P], ident_f32[:]
                    )

        def group_e(unit):
            first, count = unit
            e_grouped[unit] = work.tile(
                [P, count * P * PACK], BF16, name="e_grouped", align_bytes=64
            )
            nc.scalar.copy(
                out=e_grouped[unit][:].bitcast(F32).rearrange(
                    "p (i q u) -> p i q u", i=count, u=2
                ),
                in_=eT_ps[unit][:].rearrange("p i u q -> p i q u"),
            )

        def quantise_e(unit):
            first, count = unit
            pair, member = divmod(first, 2)
            e_codes[unit] = work.tile([P, count * P], U32, name="e_codes", align_bytes=64)
            e_scales[unit] = work.tile([P, count * P], U8, name="e_scales", align_bytes=64)
            nc.vector.quantize_mx(
                out=e_codes[unit][:].bitcast(FP8X4), scales=e_scales[unit][:],
                in_=e_grouped[unit][:],
            )
            inv_sum[unit] = small.tile([P, count], F32, name="inv_sum")
            nc.vector.reciprocal(
                out=inv_sum[unit][:], in_=row_sum[pair][:, member : member + count]
            )

        def attend(unit):
            first, count = unit
            h = first // TOKEN_TILES
            head_cols = slice(h * HD, (h + 1) * HD)
            if count == 1:
                acc[unit] = psum_s.tile([P, count, HD], F32, name="s_ps")
            else:
                acc[unit] = psum_acc.tile([P, count, HD], F32, name="acc")
            for i in range(count):
                queries = slice(i * P, (i + 1) * P)
                nc.tensor.matmul_mx(
                    out=acc[unit][:, i, :],
                    lhsT=e_codes[unit][:, queries].bitcast(FP8X4),
                    lhsT_scale=e_scales[unit][:, queries],
                    rhs=v_codes[:, head_cols].bitcast(FP8X4), rhs_scale=v_scales[:, head_cols],
                    start=True, stop=True,
                )

        def divide_and_store(unit):
            first, count = unit
            h, t = divmod(first, TOKEN_TILES)
            o_sb = results.tile([P, count, HD], F32, name="o_sb")
            nc.vector.tensor_mul(
                out=o_sb[:], in0=acc[unit][:],
                in1=inv_sum[unit][:].unsqueeze(2).to_broadcast([P, count, HD]),
            )
            nc.sync.dma_start(
                out=out_dram[:, t : t + count, h * HD : (h + 1) * HD], in_=o_sb[:]
            )

        LAG = {
            "maximum": 1, "exponential": 2, "turn": 3, "group": 4, "quantise": 6,
            "attend": 8, "divide": 9,
        }

        def units_at(n):
            if n in (TILES - 2, TILES - 1):
                return [(n, 1)]
            if 0 <= n < TILES and n % 2 == 1:
                return [(n - 1, 2)]
            return []

        def tiles_at(n):
            return [n] if 0 <= n < TILES else []

        def pipeline_round(r):
            for unit in units_at(r - LAG["attend"]):
                attend(unit)
            for n in tiles_at(r):
                if n >= 2:
                    scores(n)
            for unit in units_at(r - LAG["turn"]):
                turn_e(unit)
            for n in tiles_at(r - LAG["maximum"]):
                row_maximum(n)
            for unit in units_at(r - LAG["quantise"]):
                quantise_e(unit)
            for unit in units_at(r - LAG["divide"]):
                divide_and_store(unit)
            for n in tiles_at(r - LAG["exponential"]):
                exponential(n)
            for unit in units_at(r - LAG["group"]):
                group_e(unit)
            next_head = r // TOKEN_TILES + 1
            if r % TOKEN_TILES == 2 and next_head < HEADS:
                turn_head(next_head)
                copy_head(next_head)
            head, phase = divmod(r - 2, TOKEN_TILES)
            if phase == 2 and 0 <= head < HEADS:
                quantise_v(head)

        for n, tiles in ((0, [0]), (1, [1, 2, 3])):
            turn_first_q(tiles)
            open_scores(n)
            lay_mask(n, first=True)
            multiply(n, first=False)
        for r in range(TILES + LAG["divide"]):
            pipeline_round(r)
